import numpy as np
import ml_dtypes


def mxq(x, axis, fmt="e4m3"):
    dtype, down = {"e4m3": (ml_dtypes.float8_e4m3fn, 7), "e5m2": (ml_dtypes.float8_e5m2, 14)}[fmt]
    v = np.moveaxis(np.asarray(x, np.float32).astype(ml_dtypes.bfloat16).astype(np.float64), axis, -1)
    blocks = v.reshape(v.shape[:-1] + (-1, 32))
    amax = np.abs(blocks).max(-1, keepdims=True)
    byte = np.maximum(np.where(amax > 0, np.frexp(amax)[1] - 1 + 127, 0) - down, 1)
    scale = np.exp2(byte - 127.0)
    codes = (blocks / scale).astype(np.float32).astype(dtype).astype(np.float64)
    return np.moveaxis((codes * scale).reshape(v.shape), -1, axis)


WIDE = False


def mx_kscale(k):
    if not WIDE:
        return np.ones(k)
    levels = np.array([10, -10, 5, -5, 0])
    a = np.random.permutation(np.resize(levels, k // 512 * 4)).reshape(k // 512, 4)
    idx = np.arange(k)
    return np.exp2(a[idx // 512, idx % 128 // 32])


BF16 = ml_dtypes.bfloat16


def bf(x):
    return np.asarray(x, np.float32).astype(BF16)


def f64(x):
    return np.asarray(x).astype(np.float64)


B, T, D, H, KVH, HD = 2, 512, 2048, 16, 4, 128
HALF = HD // 2
EPS = 1e-6
ROPE_BASE = 10000.0


def zc_rmsnorm(x, scale):
    rms = np.sqrt(np.mean(x ** 2, axis=-1, keepdims=True) + EPS)
    return (1.0 + scale) * x / rms


def apply_rope(x, cos, sin):
    t = x.shape[2]
    c = cos[:t][None, None, :, :]
    s = sin[:t][None, None, :, :]
    x1, x2 = x[..., :HALF], x[..., HALF:]
    return np.concatenate([x1 * c - x2 * s, x2 * c + x1 * s], axis=-1)


def setup_inputs():
    s = mx_kscale(D)
    inv_freq = 1.0 / (ROPE_BASE ** (np.arange(0, HALF) / HALF))
    ang = np.arange(T)[:, None] * inv_freq[None, :]
    return {"kv_input": bf(np.random.standard_normal((B, T, D)) * s),
            "Wk": bf(np.random.standard_normal((D, KVH * HD)) / np.sqrt(D) / s[:, None]),
            "Wv": bf(np.random.standard_normal((D, KVH * HD)) / np.sqrt(D) / s[:, None]),
            "k_scale": bf(np.random.standard_normal(HD) * 0.2),
            "cos": bf(np.cos(ang)), "sin": bf(np.sin(ang))}


def reference(kv_input, Wk, Wv, k_scale, cos, sin):
    b = kv_input.shape[0]
    xq = mxq(f64(kv_input), 2, "e4m3")
    k = (xq @ mxq(f64(Wk), 0, "e4m3")).reshape(b, -1, KVH, HD).transpose(0, 2, 1, 3)
    v = (xq @ mxq(f64(Wv), 0, "e4m3")).reshape(b, -1, KVH, HD).transpose(0, 2, 1, 3)
    k = zc_rmsnorm(k, f64(k_scale))
    rep = H // KVH
    k = np.repeat(k, rep, axis=1)
    v = np.repeat(v, rep, axis=1)
    k = apply_rope(k, f64(cos), f64(sin))
    return k, v

@@ -1,0 +1,213 @@
+from contextlib import ExitStack
+
+import concourse.mybir as mybir
+from concourse.masks import make_identity
+
+F32 = mybir.dt.float32
+BF16 = mybir.dt.bfloat16
+U32 = mybir.dt.uint32
+U8 = mybir.dt.uint8
+FP8X4 = mybir.dt.float8_e4m3fn_x4
+ACT = mybir.ActivationFunctionType
+
+BATCH, TOKENS, FEATURES = 2, 512, 2048
+KV_HEADS, HEAD_DIM, REPEAT = 4, 128, 4
+HALF = HEAD_DIM // 2
+EPS = 1e-6
+
+P = 128
+PACK = 4
+K_PASS = P * PACK
+PASSES = FEATURES // K_PASS
+TILES = TOKENS // P
+COLS = KV_HEADS * HEAD_DIM
+PAIRS = PACK // 2
+
+FLOPS = 2 * BATCH * TOKENS * FEATURES * 2 * COLS
+
+
+def tile_multiheadattention_pb_kernel(tc, kv_input, Wk, Wv, k_scale, cos, sin, out_0, out_1):
+    nc = tc.nc
+    with ExitStack() as ctx:
+        keep = ctx.enter_context(tc.tile_pool(name="keep", bufs=1))
+        stage = ctx.enter_context(tc.tile_pool(name="stage", bufs=3))
+        small = ctx.enter_context(tc.tile_pool(name="small", bufs=4))
+        psum_t = ctx.enter_context(tc.psum_pool(name="psum_t", bufs=4))
+        psum_acc = ctx.enter_context(tc.psum_pool(name="psum_acc", bufs=4))
+
+        cos_bf = keep.tile([P, TILES, HALF], BF16)
+        sin_bf = keep.tile([P, TILES, HALF], BF16)
+        nc.scalar.dma_start(out=cos_bf[:], in_=cos.rearrange("(p j) c -> p j c", j=TILES))
+        nc.scalar.dma_start(out=sin_bf[:], in_=sin.rearrange("(p j) c -> p j c", j=TILES))
+        scale_rows = keep.tile([P, HEAD_DIM], BF16)
+        nc.vector.memset(scale_rows[:], 0.0)
+        nc.scalar.dma_start(out=scale_rows[0:1, :], in_=k_scale.rearrange("(o d) -> o d", o=1))
+
+        w_raw = {}
+        x_raw = {}
+
+        def load_weights(name, w):
+            w_raw[name] = keep.tile([P, PASSES, PACK * COLS], BF16, name="w_raw_" + name)
+            rows = w.rearrange("(c p t) n -> c p (t n)", p=P, t=PACK)
+            for c in range(PASSES):
+                nc.sync.dma_start(out=w_raw[name][:, c, :], in_=rows[c])
+
+        def load_batch(b):
+            x_raw[b] = keep.tile([P, TILES, FEATURES], BF16, name="x_raw_%d" % b)
+            rows = kv_input[b].rearrange("(p j) k -> p j k", j=TILES)
+            for j in range(TILES):
+                nc.sync.dma_start(out=x_raw[b][:, j, :], in_=rows[:, j, :])
+
+        load_weights("v", Wv)
+        load_batch(0)
+        load_batch(1)
+        load_weights("k", Wk)
+
+        ident = keep.tile([P, P], F32)
+        make_identity(nc, ident[:])
+        eps = keep.tile([P, 1], F32)
+        nc.vector.memset(eps[:], EPS)
+
+        ones = keep.tile([P, P], BF16)
+        nc.vector.memset(ones[:], 1.0)
+        spread = psum_t.tile([P, COLS], F32, tag="bank")
+        nc.tensor.matmul(out=spread[:, 0:HEAD_DIM], lhsT=ones[:], rhs=scale_rows[:], start=True, stop=True)
+        gain = keep.tile([P, 2, HALF], F32)
+        nc.vector.tensor_scalar_add(
+            out=gain[:].rearrange("p h c -> p (h c)"), in0=spread[:, 0:HEAD_DIM], scalar1=1.0
+        )
+        gain_swapped = keep.tile([P, 2, HALF], F32)
+        nc.vector.tensor_scalar_mul(out=gain_swapped[:, 0, :], in0=gain[:, 1, :], scalar1=-1.0)
+        nc.vector.tensor_copy(out=gain_swapped[:, 1, :], in_=gain[:, 0, :])
+        table_shape = [P, TILES, 2, HALF]
+        same = keep.tile(table_shape, F32)
+        other = keep.tile(table_shape, F32)
+        nc.vector.tensor_mul(
+            out=same[:],
+            in0=cos_bf[:].unsqueeze(2).to_broadcast(table_shape),
+            in1=gain[:].unsqueeze(1).to_broadcast(table_shape),
+        )
+        nc.vector.tensor_mul(
+            out=other[:],
+            in0=sin_bf[:].unsqueeze(2).to_broadcast(table_shape),
+            in1=gain_swapped[:].unsqueeze(1).to_broadcast(table_shape),
+        )
+
+        w_codes = {}
+        w_scales = {}
+
+        def quantise_weights(name):
+            w_codes[name] = keep.tile([P, PASSES, COLS], U32, name="w_codes_" + name, align_bytes=64)
+            w_scales[name] = keep.tile([P, PASSES, COLS], U8, name="w_scales_" + name, align_bytes=64)
+            for c in range(PASSES):
+                w_grouped = stage.tile([P, COLS * PACK], BF16, align_bytes=64)
+                nc.vector.tensor_copy(
+                    out=w_grouped[:].rearrange("p (q i t) -> p q t i", i=4, t=PACK),
+                    in_=w_raw[name][:, c, :].rearrange("p (t q i) -> p q t i", t=PACK, i=4),
+                )
+                nc.vector.quantize_mx(
+                    out=w_codes[name][:, c, :].bitcast(FP8X4),
+                    scales=w_scales[name][:, c, :],
+                    in_=w_grouped[:],
+                )
+
+        x_codes = keep.tile([P, BATCH, TILES, PASSES * P], U32, align_bytes=64)
+        x_scales = keep.tile([P, BATCH, TILES, PASSES * P], U8, align_bytes=64)
+
+        def quantise_tokens(b, j):
+            words = x_raw[b][:, j, :].bitcast(F32).rearrange("p (c i u) -> p c u i", c=PASSES, u=PAIRS)
+            x_grouped = stage.tile([P, PASSES * P * PACK], BF16, align_bytes=64)
+            grouped_words = x_grouped[:].bitcast(F32).rearrange("p (c m u) -> p c m u", c=PASSES, u=PAIRS)
+            passes_per_bank = COLS // (PAIRS * P)
+            for c0 in range(0, PASSES, passes_per_bank):
+                flipped = psum_t.tile([P, passes_per_bank, PAIRS, P], F32, tag="bank")
+                for cc in range(passes_per_bank):
+                    for u in range(PAIRS):
+                        nc.tensor.transpose(flipped[:, cc, u, :], words[:, c0 + cc, u, :], ident[:])
+                nc.scalar.copy(
+                    out=grouped_words[:, c0 : c0 + passes_per_bank, :, :],
+                    in_=flipped[:].rearrange("p c u m -> p c m u"),
+                )
+            nc.vector.quantize_mx(
+                out=x_codes[:, b, j, :].bitcast(FP8X4), scales=x_scales[:, b, j, :], in_=x_grouped[:]
+            )
+
+        def project(name, b, j):
+            acc = psum_acc.tile([P, COLS], F32)
+            for c in range(PASSES):
+                tokens = slice(c * P, (c + 1) * P)
+                nc.tensor.matmul_mx(
+                    out=acc[:],
+                    lhsT=x_codes[:, b, j, tokens].bitcast(FP8X4),
+                    lhsT_scale=x_scales[:, b, j, tokens],
+                    rhs=w_codes[name][:, c, :].bitcast(FP8X4),
+                    rhs_scale=w_scales[name][:, c, :],
+                    start=(c == 0),
+                    stop=(c == PASSES - 1),
+                )
+            return acc
+
+        def store_heads(out, b, result):
+            for g in range(KV_HEADS):
+                for r in range(REPEAT):
+                    nc.sync.dma_start(
+                        out=out[b, g * REPEAT + r].rearrange("(p j) d -> p (j d)", j=TILES),
+                        in_=result[:, g, :, :].rearrange("p j d -> p (j d)"),
+                    )
+
+        def values(b, j, result):
+            acc = project("v", b, j)
+            nc.scalar.copy(out=result[:, :, j, :], in_=acc[:].rearrange("p (g d) -> p g d", g=KV_HEADS))
+
+        def keys(b, j, result):
+            acc = project("k", b, j)
+            heads = acc[:].rearrange("p (g d) -> p g d", g=KV_HEADS)
+            sum_sq = small.tile([P, KV_HEADS], F32)
+            for g in range(KV_HEADS):
+                squares = stage.tile([P, HEAD_DIM], F32)
+                nc.scalar.activation(
+                    out=squares[:], in_=heads[:, g, :], func=ACT.Square, accum_out=sum_sq[:, g : g + 1]
+                )
+            rms = small.tile([P, KV_HEADS], F32)
+            nc.scalar.activation(out=rms[:], in_=sum_sq[:], func=ACT.Sqrt, bias=eps[:], scale=1.0 / HEAD_DIM)
+            inv_rms = small.tile([P, KV_HEADS], F32)
+            nc.vector.reciprocal(out=inv_rms[:], in_=rms[:])
+            normed = stage.tile([P, KV_HEADS, 2, HALF], F32)
+            for g in range(KV_HEADS):
+                nc.scalar.activation(
+                    out=normed[:, g, :, :].rearrange("p h c -> p (h c)"),
+                    in_=heads[:, g, :],
+                    func=ACT.Copy,
+                    scale=inv_rms[:, g : g + 1],
+                )
+            head_shape = [P, KV_HEADS, 2, HALF]
+            straight = stage.tile(head_shape, F32)
+            nc.vector.tensor_mul(
+                out=straight[:], in0=normed[:], in1=same[:, j, :, :].unsqueeze(1).to_broadcast(head_shape)
+            )
+            crossed = stage.tile(head_shape, F32)
+            for h in range(2):
+                nc.vector.tensor_mul(
+                    out=crossed[:, :, h, :],
+                    in0=normed[:, :, 1 - h, :],
+                    in1=other[:, j, h, :].unsqueeze(1).to_broadcast([P, KV_HEADS, HALF]),
+                )
+            nc.vector.tensor_add(
+                out=result[:, :, j, :],
+                in0=straight[:].rearrange("p g h c -> p g (h c)"),
+                in1=crossed[:].rearrange("p g h c -> p g (h c)"),
+            )
+
+        quantise_weights("v")
+        for b in range(BATCH):
+            v_result = keep.tile([P, KV_HEADS, TILES, HEAD_DIM], F32, name="v_result_%d" % b)
+            for j in range(TILES):
+                quantise_tokens(b, j)
+                values(b, j, v_result)
+            store_heads(out_1, b, v_result)
+        quantise_weights("k")
+        for b in range(BATCH):
+            k_result = keep.tile([P, KV_HEADS, TILES, HEAD_DIM], F32, name="k_result_%d" % b)
+            for j in range(TILES):
+                keys(b, j, k_result)
+            store_heads(out_0, b, k_result)

@@ -32,6 +32,7 @@ def tile_multiheadattention_pb_kernel(tc, kv_input, Wk, Wv, k_scale, cos, sin, o
         keep = ctx.enter_context(tc.tile_pool(name="keep", bufs=1))
         stage = ctx.enter_context(tc.tile_pool(name="stage", bufs=3))
         small = ctx.enter_context(tc.tile_pool(name="small", bufs=4))
+        results = ctx.enter_context(tc.tile_pool(name="results", bufs=1))
         psum_t = ctx.enter_context(tc.psum_pool(name="psum_t", bufs=4))
         psum_acc = ctx.enter_context(tc.psum_pool(name="psum_acc", bufs=4))
 
@@ -132,82 +133,75 @@ def tile_multiheadattention_pb_kernel(tc, kv_input, Wk, Wv, k_scale, cos, sin, o
                 out=x_codes[:, b, j, :].bitcast(FP8X4), scales=x_scales[:, b, j, :], in_=x_grouped[:]
             )
 
-        def project(name, b, j):
-            acc = psum_acc.tile([P, COLS], F32)
-            for c in range(PASSES):
-                tokens = slice(c * P, (c + 1) * P)
-                nc.tensor.matmul_mx(
-                    out=acc[:],
-                    lhsT=x_codes[:, b, j, tokens].bitcast(FP8X4),
-                    lhsT_scale=x_scales[:, b, j, tokens],
-                    rhs=w_codes[name][:, c, :].bitcast(FP8X4),
-                    rhs_scale=w_scales[name][:, c, :],
-                    start=(c == 0),
-                    stop=(c == PASSES - 1),
-                )
+        def project(name, b, g):
+            acc = psum_acc.tile([P, TILES, HEAD_DIM], F32)
+            head_cols = slice(g * HEAD_DIM, (g + 1) * HEAD_DIM)
+            for j in range(TILES):
+                for c in range(PASSES):
+                    tokens = slice(c * P, (c + 1) * P)
+                    nc.tensor.matmul_mx(
+                        out=acc[:, j, :],
+                        lhsT=x_codes[:, b, j, tokens].bitcast(FP8X4),
+                        lhsT_scale=x_scales[:, b, j, tokens],
+                        rhs=w_codes[name][:, c, head_cols].bitcast(FP8X4),
+                        rhs_scale=w_scales[name][:, c, head_cols],
+                        start=(c == 0),
+                        stop=(c == PASSES - 1),
+                    )
             return acc
 
-        def store_heads(out, b, result):
-            for g in range(KV_HEADS):
-                for r in range(REPEAT):
-                    nc.sync.dma_start(
-                        out=out[b, g * REPEAT + r].rearrange("(p j) d -> p (j d)", j=TILES),
-                        in_=result[:, g, :, :].rearrange("p j d -> p (j d)"),
-                    )
+        def store_head(out, b, g, result):
+            for r in range(REPEAT):
+                nc.sync.dma_start(
+                    out=out[b, g * REPEAT + r].rearrange("(p j) d -> p (j d)", j=TILES), in_=result
+                )
 
-        def values(b, j, result):
-            acc = project("v", b, j)
-            nc.scalar.copy(out=result[:, :, j, :], in_=acc[:].rearrange("p (g d) -> p g d", g=KV_HEADS))
+        def values(b, g):
+            acc = project("v", b, g)
+            v_result = results.tile([P, TILES * HEAD_DIM], F32, name="v_result_%d_%d" % (b, g))
+            nc.scalar.copy(out=v_result[:], in_=acc[:].rearrange("p j d -> p (j d)"))
+            store_head(out_1, b, g, v_result[:])
 
-        def keys(b, j, result):
-            acc = project("k", b, j)
-            heads = acc[:].rearrange("p (g d) -> p g d", g=KV_HEADS)
-            sum_sq = small.tile([P, KV_HEADS], F32)
-            for g in range(KV_HEADS):
+        def keys(b, g):
+            acc = project("k", b, g)
+            sum_sq = small.tile([P, TILES], F32)
+            for j in range(TILES):
                 squares = stage.tile([P, HEAD_DIM], F32)
                 nc.scalar.activation(
-                    out=squares[:], in_=heads[:, g, :], func=ACT.Square, accum_out=sum_sq[:, g : g + 1]
+                    out=squares[:], in_=acc[:, j, :], func=ACT.Square, accum_out=sum_sq[:, j : j + 1]
                 )
-            rms = small.tile([P, KV_HEADS], F32)
+            rms = small.tile([P, TILES], F32)
             nc.scalar.activation(out=rms[:], in_=sum_sq[:], func=ACT.Sqrt, bias=eps[:], scale=1.0 / HEAD_DIM)
-            inv_rms = small.tile([P, KV_HEADS], F32)
+            inv_rms = small.tile([P, TILES], F32)
             nc.vector.reciprocal(out=inv_rms[:], in_=rms[:])
-            normed = stage.tile([P, KV_HEADS, 2, HALF], F32)
-            for g in range(KV_HEADS):
+            normed = stage.tile(table_shape, F32)
+            for j in range(TILES):
                 nc.scalar.activation(
-                    out=normed[:, g, :, :].rearrange("p h c -> p (h c)"),
-                    in_=heads[:, g, :],
+                    out=normed[:, j, :, :].rearrange("p h c -> p (h c)"),
+                    in_=acc[:, j, :],
                     func=ACT.Copy,
-                    scale=inv_rms[:, g : g + 1],
+                    scale=inv_rms[:, j : j + 1],
                 )
-            head_shape = [P, KV_HEADS, 2, HALF]
-            straight = stage.tile(head_shape, F32)
-            nc.vector.tensor_mul(
-                out=straight[:], in0=normed[:], in1=same[:, j, :, :].unsqueeze(1).to_broadcast(head_shape)
-            )
-            crossed = stage.tile(head_shape, F32)
+            straight = stage.tile(table_shape, F32)
+            nc.vector.tensor_mul(out=straight[:], in0=normed[:], in1=same[:])
+            crossed = stage.tile(table_shape, F32)
             for h in range(2):
-                nc.vector.tensor_mul(
-                    out=crossed[:, :, h, :],
-                    in0=normed[:, :, 1 - h, :],
-                    in1=other[:, j, h, :].unsqueeze(1).to_broadcast([P, KV_HEADS, HALF]),
-                )
+                nc.vector.tensor_mul(out=crossed[:, :, h, :], in0=normed[:, :, 1 - h, :], in1=other[:, :, h, :])
+            k_result = results.tile([P, TILES * HEAD_DIM], F32, name="k_result_%d_%d" % (b, g))
             nc.vector.tensor_add(
-                out=result[:, :, j, :],
-                in0=straight[:].rearrange("p g h c -> p g (h c)"),
-                in1=crossed[:].rearrange("p g h c -> p g (h c)"),
+                out=k_result[:],
+                in0=straight[:].rearrange("p j h c -> p (j h c)"),
+                in1=crossed[:].rearrange("p j h c -> p (j h c)"),
             )
+            store_head(out_0, b, g, k_result[:])
 
         quantise_weights("v")
         for b in range(BATCH):
-            v_result = keep.tile([P, KV_HEADS, TILES, HEAD_DIM], F32, name="v_result_%d" % b)
             for j in range(TILES):
                 quantise_tokens(b, j)
-                values(b, j, v_result)
-            store_heads(out_1, b, v_result)
+            for g in range(KV_HEADS):
+                values(b, g)
         quantise_weights("k")
         for b in range(BATCH):
-            k_result = keep.tile([P, KV_HEADS, TILES, HEAD_DIM], F32, name="k_result_%d" % b)
-            for j in range(TILES):
-                keys(b, j, k_result)
-            store_heads(out_0, b, k_result)
+            for g in range(KV_HEADS):
+                keys(b, g)

@@ -151,10 +151,8 @@ def tile_multiheadattention_pb_kernel(tc, kv_input, Wk, Wv, k_scale, cos, sin, o
             return acc
 
         def store_head(out, b, g, result):
-            for r in range(REPEAT):
-                nc.sync.dma_start(
-                    out=out[b, g * REPEAT + r].rearrange("(p j) d -> p (j d)", j=TILES), in_=result
-                )
+            served = out[b, g * REPEAT : (g + 1) * REPEAT].rearrange("r (p j) d -> p r (j d)", j=TILES)
+            nc.sync.dma_start(out=served, in_=result.unsqueeze(1).to_broadcast([P, REPEAT, TILES * HEAD_DIM]))
 
         def values(b, g):
             acc = project("v", b, g)

@@ -33,8 +33,7 @@ def tile_multiheadattention_pb_kernel(tc, kv_input, Wk, Wv, k_scale, cos, sin, o
         stage = ctx.enter_context(tc.tile_pool(name="stage", bufs=3))
         small = ctx.enter_context(tc.tile_pool(name="small", bufs=4))
         results = ctx.enter_context(tc.tile_pool(name="results", bufs=1))
-        psum_t = ctx.enter_context(tc.psum_pool(name="psum_t", bufs=4))
-        psum_acc = ctx.enter_context(tc.psum_pool(name="psum_acc", bufs=4))
+        psum = ctx.enter_context(tc.psum_pool(name="psum", bufs=8))
 
         cos_bf = keep.tile([P, TILES, HALF], BF16)
         sin_bf = keep.tile([P, TILES, HALF], BF16)
@@ -68,10 +67,12 @@ def tile_multiheadattention_pb_kernel(tc, kv_input, Wk, Wv, k_scale, cos, sin, o
         make_identity(nc, ident[:])
         eps = keep.tile([P, 1], F32)
         nc.vector.memset(eps[:], EPS)
+        warm = keep.tile([P, 1], F32)
+        nc.scalar.activation(out=warm[:], in_=eps[:], func=ACT.Abs_reciprocal_sqrt)
 
         ones = keep.tile([P, P], BF16)
         nc.vector.memset(ones[:], 1.0)
-        spread = psum_t.tile([P, COLS], F32, tag="bank")
+        spread = psum.tile([P, COLS], F32, tag="bank")
         nc.tensor.matmul(out=spread[:, 0:HEAD_DIM], lhsT=ones[:], rhs=scale_rows[:], start=True, stop=True)
         gain = keep.tile([P, 2, HALF], F32)
         nc.vector.tensor_scalar_add(
@@ -83,34 +84,45 @@ def tile_multiheadattention_pb_kernel(tc, kv_input, Wk, Wv, k_scale, cos, sin, o
         table_shape = [P, TILES, 2, HALF]
         same = keep.tile(table_shape, F32)
         other = keep.tile(table_shape, F32)
-        nc.vector.tensor_mul(
-            out=same[:],
-            in0=cos_bf[:].unsqueeze(2).to_broadcast(table_shape),
-            in1=gain[:].unsqueeze(1).to_broadcast(table_shape),
-        )
-        nc.vector.tensor_mul(
-            out=other[:],
-            in0=sin_bf[:].unsqueeze(2).to_broadcast(table_shape),
-            in1=gain_swapped[:].unsqueeze(1).to_broadcast(table_shape),
-        )
+
+        def build_tables():
+            nc.vector.tensor_mul(
+                out=same[:],
+                in0=cos_bf[:].unsqueeze(2).to_broadcast(table_shape),
+                in1=gain[:].unsqueeze(1).to_broadcast(table_shape),
+            )
+            nc.vector.tensor_mul(
+                out=other[:],
+                in0=sin_bf[:].unsqueeze(2).to_broadcast(table_shape),
+                in1=gain_swapped[:].unsqueeze(1).to_broadcast(table_shape),
+            )
 
         w_codes = {}
         w_scales = {}
+        w_grouped = {}
+
+        def group_weights(name, c):
+            w_grouped[name, c] = stage.tile([P, COLS * PACK], BF16, align_bytes=64, tag="w_grouped", name="w_grouped")
+            nc.vector.tensor_copy(
+                out=w_grouped[name, c][:].rearrange("p (q i t) -> p q t i", i=4, t=PACK),
+                in_=w_raw[name][:, c, :].rearrange("p (t q i) -> p q t i", t=PACK, i=4),
+            )
+
+        def quantise_weights_pass(name, c):
+            nc.vector.quantize_mx(
+                out=w_codes[name][:, c, :].bitcast(FP8X4),
+                scales=w_scales[name][:, c, :],
+                in_=w_grouped[name, c][:],
+            )
 
         def quantise_weights(name):
             w_codes[name] = keep.tile([P, PASSES, COLS], U32, name="w_codes_" + name, align_bytes=64)
             w_scales[name] = keep.tile([P, PASSES, COLS], U8, name="w_scales_" + name, align_bytes=64)
+            group_weights(name, 0)
             for c in range(PASSES):
-                w_grouped = stage.tile([P, COLS * PACK], BF16, align_bytes=64)
-                nc.vector.tensor_copy(
-                    out=w_grouped[:].rearrange("p (q i t) -> p q t i", i=4, t=PACK),
-                    in_=w_raw[name][:, c, :].rearrange("p (t q i) -> p q t i", t=PACK, i=4),
-                )
-                nc.vector.quantize_mx(
-                    out=w_codes[name][:, c, :].bitcast(FP8X4),
-                    scales=w_scales[name][:, c, :],
-                    in_=w_grouped[:],
-                )
+                if c + 1 < PASSES:
+                    group_weights(name, c + 1)
+                quantise_weights_pass(name, c)
 
         x_codes = keep.tile([P, BATCH, TILES, PASSES * P], U32, align_bytes=64)
         x_scales = keep.tile([P, BATCH, TILES, PASSES * P], U8, align_bytes=64)
@@ -121,7 +133,7 @@ def tile_multiheadattention_pb_kernel(tc, kv_input, Wk, Wv, k_scale, cos, sin, o
             grouped_words = x_grouped[:].bitcast(F32).rearrange("p (c m u) -> p c m u", c=PASSES, u=PAIRS)
             passes_per_bank = COLS // (PAIRS * P)
             for c0 in range(0, PASSES, passes_per_bank):
-                flipped = psum_t.tile([P, passes_per_bank, PAIRS, P], F32, tag="bank")
+                flipped = psum.tile([P, passes_per_bank, PAIRS, P], F32, tag="bank")
                 for cc in range(passes_per_bank):
                     for u in range(PAIRS):
                         nc.tensor.transpose(flipped[:, cc, u, :], words[:, c0 + cc, u, :], ident[:])
@@ -134,7 +146,7 @@ def tile_multiheadattention_pb_kernel(tc, kv_input, Wk, Wv, k_scale, cos, sin, o
             )
 
         def project(name, b, g):
-            acc = psum_acc.tile([P, TILES, HEAD_DIM], F32)
+            acc = psum.tile([P, TILES, HEAD_DIM], F32, tag="bank")
             head_cols = slice(g * HEAD_DIM, (g + 1) * HEAD_DIM)
             for j in range(TILES):
                 for c in range(PASSES):
@@ -160,46 +172,73 @@ def tile_multiheadattention_pb_kernel(tc, kv_input, Wk, Wv, k_scale, cos, sin, o
             nc.scalar.copy(out=v_result[:], in_=acc[:].rearrange("p j d -> p (j d)"))
             store_head(out_1, b, g, v_result[:])
 
-        def keys(b, g):
+        k_acc = {}
+        k_inv = {}
+        k_straight = {}
+        k_crossed = {}
+        k_sum = {}
+
+        def keys_product(b, g):
             acc = project("k", b, g)
+            k_acc[b, g] = acc
             sum_sq = small.tile([P, TILES], F32)
             for j in range(TILES):
                 squares = stage.tile([P, HEAD_DIM], F32)
                 nc.scalar.activation(
                     out=squares[:], in_=acc[:, j, :], func=ACT.Square, accum_out=sum_sq[:, j : j + 1]
                 )
-            rms = small.tile([P, TILES], F32)
-            nc.scalar.activation(out=rms[:], in_=sum_sq[:], func=ACT.Sqrt, bias=eps[:], scale=1.0 / HEAD_DIM)
             inv_rms = small.tile([P, TILES], F32)
-            nc.vector.reciprocal(out=inv_rms[:], in_=rms[:])
-            normed = stage.tile(table_shape, F32)
-            for j in range(TILES):
-                nc.scalar.activation(
-                    out=normed[:, j, :, :].rearrange("p h c -> p (h c)"),
-                    in_=acc[:, j, :],
-                    func=ACT.Copy,
-                    scale=inv_rms[:, j : j + 1],
-                )
+            nc.scalar.activation(
+                out=inv_rms[:], in_=sum_sq[:], func=ACT.Abs_reciprocal_sqrt, bias=eps[:], scale=1.0 / HEAD_DIM
+            )
+            k_inv[b, g] = inv_rms
+            halves = acc[:].rearrange("p j (h c) -> p j h c", h=2)
             straight = stage.tile(table_shape, F32)
-            nc.vector.tensor_mul(out=straight[:], in0=normed[:], in1=same[:])
+            nc.vector.tensor_mul(out=straight[:], in0=halves, in1=same[:])
             crossed = stage.tile(table_shape, F32)
             for h in range(2):
-                nc.vector.tensor_mul(out=crossed[:, :, h, :], in0=normed[:, :, 1 - h, :], in1=other[:, :, h, :])
-            k_result = results.tile([P, TILES * HEAD_DIM], F32, name="k_result_%d_%d" % (b, g))
-            nc.vector.tensor_add(
-                out=k_result[:],
-                in0=straight[:].rearrange("p j h c -> p (j h c)"),
-                in1=crossed[:].rearrange("p j h c -> p (j h c)"),
+                nc.vector.tensor_mul(out=crossed[:, :, h, :], in0=halves[:, :, 1 - h, :], in1=other[:, :, h, :])
+            k_straight[b, g] = straight
+            k_crossed[b, g] = crossed
+
+        def keys_sum(b, g):
+            roped = stage.tile([P, TILES, HEAD_DIM], F32)
+            nc.gpsimd.tensor_tensor(
+                out=roped[:].rearrange("p j d -> p (j d)"),
+                in0=k_straight[b, g][:].rearrange("p j h c -> p (j h c)"),
+                in1=k_crossed[b, g][:].rearrange("p j h c -> p (j h c)"),
+                op=mybir.AluOpType.add,
             )
-            store_head(out_0, b, g, k_result[:])
+            k_sum[b, g] = roped
+
+        def keys_finish(b, g):
+            k_result = results.tile([P, TILES, HEAD_DIM], F32, name="k_result_%d_%d" % (b, g))
+            for j in range(TILES):
+                nc.scalar.activation(
+                    out=k_result[:, j, :], in_=k_sum[b, g][:, j, :], func=ACT.Copy, scale=k_inv[b, g][:, j : j + 1]
+                )
+            store_head(out_0, b, g, k_result[:].rearrange("p j d -> p (j d)"))
 
         quantise_weights("v")
-        for b in range(BATCH):
-            for j in range(TILES):
-                quantise_tokens(b, j)
-            for g in range(KV_HEADS):
-                values(b, g)
+        for j in range(TILES):
+            quantise_tokens(0, j)
+        build_tables()
+        values(0, 0)
+        values(0, 1)
+        quantise_tokens(1, 0)
+        quantise_tokens(1, 1)
+        values(0, 2)
+        quantise_tokens(1, 2)
+        quantise_tokens(1, 3)
+        values(0, 3)
         quantise_weights("k")
-        for b in range(BATCH):
-            for g in range(KV_HEADS):
-                keys(b, g)
+        for g in range(KV_HEADS):
+            values(1, g)
+        heads = [(b, g) for b in range(BATCH) for g in range(KV_HEADS)]
+        for n in range(len(heads) + 2):
+            if n < len(heads):
+                keys_product(*heads[n])
+            if 1 <= n <= len(heads):
+                keys_sum(*heads[n - 1])
+            if n >= 2:
+                keys_finish(*heads[n - 2])

@@ -34,6 +34,7 @@ def tile_multiheadattention_pb_kernel(tc, kv_input, Wk, Wv, k_scale, cos, sin, o
         small = ctx.enter_context(tc.tile_pool(name="small", bufs=4))
         results = ctx.enter_context(tc.tile_pool(name="results", bufs=1))
         psum = ctx.enter_context(tc.psum_pool(name="psum", bufs=8))
+        ctx.enter_context(tc.manual_schedule())
 
         cos_bf = keep.tile([P, TILES, HALF], BF16)
         sin_bf = keep.tile([P, TILES, HALF], BF16)
@@ -72,20 +73,20 @@ def tile_multiheadattention_pb_kernel(tc, kv_input, Wk, Wv, k_scale, cos, sin, o
 
         ones = keep.tile([P, P], BF16)
         nc.vector.memset(ones[:], 1.0)
-        spread = psum.tile([P, COLS], F32, tag="bank")
-        nc.tensor.matmul(out=spread[:, 0:HEAD_DIM], lhsT=ones[:], rhs=scale_rows[:], start=True, stop=True)
         gain = keep.tile([P, 2, HALF], F32)
-        nc.vector.tensor_scalar_add(
-            out=gain[:].rearrange("p h c -> p (h c)"), in0=spread[:, 0:HEAD_DIM], scalar1=1.0
-        )
         gain_swapped = keep.tile([P, 2, HALF], F32)
-        nc.vector.tensor_scalar_mul(out=gain_swapped[:, 0, :], in0=gain[:, 1, :], scalar1=-1.0)
-        nc.vector.tensor_copy(out=gain_swapped[:, 1, :], in_=gain[:, 0, :])
         table_shape = [P, TILES, 2, HALF]
         same = keep.tile(table_shape, F32)
         other = keep.tile(table_shape, F32)
 
         def build_tables():
+            spread = psum.tile([P, COLS], F32, tag="bank")
+            nc.tensor.matmul(out=spread[:, 0:HEAD_DIM], lhsT=ones[:], rhs=scale_rows[:], start=True, stop=True)
+            nc.vector.tensor_scalar_add(
+                out=gain[:].rearrange("p h c -> p (h c)"), in0=spread[:, 0:HEAD_DIM], scalar1=1.0
+            )
+            nc.vector.tensor_scalar_mul(out=gain_swapped[:, 0, :], in0=gain[:, 1, :], scalar1=-1.0)
+            nc.vector.tensor_copy(out=gain_swapped[:, 1, :], in_=gain[:, 0, :])
             nc.vector.tensor_mul(
                 out=same[:],
                 in0=cos_bf[:].unsqueeze(2).to_broadcast(table_shape),
@@ -115,9 +116,11 @@ def tile_multiheadattention_pb_kernel(tc, kv_input, Wk, Wv, k_scale, cos, sin, o
                 in_=w_grouped[name, c][:],
             )
 
-        def quantise_weights(name):
+        for name in ("v", "k"):
             w_codes[name] = keep.tile([P, PASSES, COLS], U32, name="w_codes_" + name, align_bytes=64)
             w_scales[name] = keep.tile([P, PASSES, COLS], U8, name="w_scales_" + name, align_bytes=64)
+
+        def quantise_weights(name):
             group_weights(name, 0)
             for c in range(PASSES):
                 if c + 1 < PASSES:
@@ -127,22 +130,31 @@ def tile_multiheadattention_pb_kernel(tc, kv_input, Wk, Wv, k_scale, cos, sin, o
         x_codes = keep.tile([P, BATCH, TILES, PASSES * P], U32, align_bytes=64)
         x_scales = keep.tile([P, BATCH, TILES, PASSES * P], U8, align_bytes=64)
 
-        def quantise_tokens(b, j):
+        passes_per_bank = COLS // (PAIRS * P)
+        x_flipped = {}
+        x_grouped = {}
+
+        def flip_tokens(b, j):
             words = x_raw[b][:, j, :].bitcast(F32).rearrange("p (c i u) -> p c u i", c=PASSES, u=PAIRS)
-            x_grouped = stage.tile([P, PASSES * P * PACK], BF16, align_bytes=64)
-            grouped_words = x_grouped[:].bitcast(F32).rearrange("p (c m u) -> p c m u", c=PASSES, u=PAIRS)
-            passes_per_bank = COLS // (PAIRS * P)
             for c0 in range(0, PASSES, passes_per_bank):
                 flipped = psum.tile([P, passes_per_bank, PAIRS, P], F32, tag="bank")
+                x_flipped[b, j, c0] = flipped
                 for cc in range(passes_per_bank):
                     for u in range(PAIRS):
                         nc.tensor.transpose(flipped[:, cc, u, :], words[:, c0 + cc, u, :], ident[:])
+
+        def group_tokens(b, j):
+            x_grouped[b, j] = stage.tile([P, PASSES * P * PACK], BF16, align_bytes=64, tag="x_grouped", name="x_grouped")
+            grouped_words = x_grouped[b, j][:].bitcast(F32).rearrange("p (c m u) -> p c m u", c=PASSES, u=PAIRS)
+            for c0 in range(0, PASSES, passes_per_bank):
                 nc.scalar.copy(
                     out=grouped_words[:, c0 : c0 + passes_per_bank, :, :],
-                    in_=flipped[:].rearrange("p c u m -> p c m u"),
+                    in_=x_flipped[b, j, c0][:].rearrange("p c u m -> p c m u"),
                 )
+
+        def quantise_tokens(b, j):
             nc.vector.quantize_mx(
-                out=x_codes[:, b, j, :].bitcast(FP8X4), scales=x_scales[:, b, j, :], in_=x_grouped[:]
+                out=x_codes[:, b, j, :].bitcast(FP8X4), scales=x_scales[:, b, j, :], in_=x_grouped[b, j][:]
             )
 
         def project(name, b, g):
@@ -166,11 +178,19 @@ def tile_multiheadattention_pb_kernel(tc, kv_input, Wk, Wv, k_scale, cos, sin, o
             served = out[b, g * REPEAT : (g + 1) * REPEAT].rearrange("r (p j) d -> p r (j d)", j=TILES)
             nc.sync.dma_start(out=served, in_=result.unsqueeze(1).to_broadcast([P, REPEAT, TILES * HEAD_DIM]))
 
-        def values(b, g):
-            acc = project("v", b, g)
+        v_acc = {}
+
+        def values_product(b, g):
+            v_acc[b, g] = project("v", b, g)
+
+        def values_finish(b, g):
             v_result = results.tile([P, TILES * HEAD_DIM], F32, name="v_result_%d_%d" % (b, g))
-            nc.scalar.copy(out=v_result[:], in_=acc[:].rearrange("p j d -> p (j d)"))
+            nc.scalar.copy(out=v_result[:], in_=v_acc[b, g][:].rearrange("p j d -> p (j d)"))
             store_head(out_1, b, g, v_result[:])
+
+        def values(b, g):
+            values_product(b, g)
+            values_finish(b, g)
 
         k_acc = {}
         k_inv = {}
@@ -221,15 +241,26 @@ def tile_multiheadattention_pb_kernel(tc, kv_input, Wk, Wv, k_scale, cos, sin, o
 
         quantise_weights("v")
         for j in range(TILES):
+            flip_tokens(0, j)
+            group_tokens(0, j)
             quantise_tokens(0, j)
-        build_tables()
-        values(0, 0)
-        values(0, 1)
+        flip_tokens(1, 0)
+        flip_tokens(1, 1)
+        group_tokens(1, 0)
+        values_product(0, 0)
+        values_finish(0, 0)
+        group_tokens(1, 1)
         quantise_tokens(1, 0)
         quantise_tokens(1, 1)
-        values(0, 2)
+        values(0, 1)
+        build_tables()
+        flip_tokens(1, 2)
+        group_tokens(1, 2)
+        flip_tokens(1, 3)
+        group_tokens(1, 3)
         quantise_tokens(1, 2)
         quantise_tokens(1, 3)
+        values(0, 2)
         values(0, 3)
         quantise_weights("k")
         for g in range(KV_HEADS):

@@ -20,6 +20,9 @@ PACK = 4
 K_PASS = P * PACK
 PASSES = FEATURES // K_PASS
 TILES = TOKENS // P
+COPIES = 2
+PER_COPY = P // COPIES
+SLOTS = TOKENS // PER_COPY
 COLS = KV_HEADS * HEAD_DIM
 PAIRS = PACK // 2
 
@@ -231,13 +234,54 @@ def tile_multiheadattention_pb_kernel(tc, kv_input, Wk, Wv, k_scale, cos, sin, o
             )
             k_sum[b, g] = roped
 
-        def keys_finish(b, g):
-            k_result = results.tile([P, TILES, HEAD_DIM], F32, name="k_result_%d_%d" % (b, g))
+        k_scaled = {}
+        k_across = {}
+
+        def keys_scale(b, g, scaled):
             for j in range(TILES):
                 nc.scalar.activation(
-                    out=k_result[:, j, :], in_=k_sum[b, g][:, j, :], func=ACT.Copy, scale=k_inv[b, g][:, j : j + 1]
+                    out=scaled[:, j, :],
+                    in_=k_sum[b, g][:, j, :],
+                    func=ACT.Copy,
+                    scale=k_inv[b, g][:, j : j + 1],
                 )
+
+        def keys_finish(b, g):
+            k_result = results.tile([P, TILES, HEAD_DIM], F32, name="k_result_%d_%d" % (b, g))
+            keys_scale(b, g, k_result)
             store_head(out_0, b, g, k_result[:].rearrange("p j d -> p (j d)"))
+
+        def keys_scale_double(b, g):
+            k_scaled[b, g] = stage.tile([P, TILES, HEAD_DIM], F32, tag="k_scaled", name="k_scaled")
+            keys_scale(b, g, k_scaled[b, g])
+
+        def keys_across(b, g):
+            turned = psum.tile([P, TILES, P], F32, tag="bank")
+            for j in range(TILES):
+                nc.tensor.transpose(turned[:, j, :], k_scaled[b, g][:, j, :], ident[:])
+            k_across[b, g] = stage.tile([P, 2, TILES, COPIES, PER_COPY], F32, tag="k_across", name="k_across")
+            for h in range(2):
+                nc.vector.tensor_copy(
+                    out=k_across[b, g][:, h],
+                    in_=turned[:]
+                    .rearrange("p j (i h) -> p h j i", h=2)[:, h]
+                    .unsqueeze(2)
+                    .to_broadcast([P, TILES, COPIES, PER_COPY]),
+                )
+
+        def keys_back(b, g):
+            result = results.tile([P, SLOTS, HEAD_DIM], F32, name="k_result_%d_%d" % (b, g))
+            for h, copy in enumerate((nc.scalar.copy, nc.vector.tensor_copy)):
+                back = psum.tile([P, TILES, HEAD_DIM], F32, tag="bank")
+                for j in range(TILES):
+                    nc.tensor.transpose(back[:, j, :], k_across[b, g][:, h, j].rearrange("p r i -> p (r i)"), ident[:])
+                copy(out=result[:, h * TILES : (h + 1) * TILES, :], in_=back[:])
+            served = out_0[b, g * REPEAT : (g + 1) * REPEAT].rearrange("(q r) t d -> q (r t d)", r=COPIES)
+            run = SLOTS * HEAD_DIM
+            nc.sync.dma_start(
+                out=served.rearrange("q (p e) -> p q e", e=run),
+                in_=result[:].rearrange("p j d -> p (j d)").unsqueeze(1).to_broadcast([P, REPEAT // COPIES, run]),
+            )
 
         quantise_weights("v")
         for j in range(TILES):
@@ -265,11 +309,18 @@ def tile_multiheadattention_pb_kernel(tc, kv_input, Wk, Wv, k_scale, cos, sin, o
         quantise_weights("k")
         for g in range(KV_HEADS):
             values(1, g)
-        heads = [(b, g) for b in range(BATCH) for g in range(KV_HEADS)]
-        for n in range(len(heads) + 2):
+        heads = [(b, g) for g in range(KV_HEADS) for b in range(BATCH)]
+        def doubled(head):
+            return head[0] == 1
+
+        for n in range(len(heads) + 4):
             if n < len(heads):
                 keys_product(*heads[n])
             if 1 <= n <= len(heads):
                 keys_sum(*heads[n - 1])
-            if n >= 2:
-                keys_finish(*heads[n - 2])
+            if 2 <= n < len(heads) + 2:
+                (keys_scale_double if doubled(heads[n - 2]) else keys_finish)(*heads[n - 2])
+            if 0 <= n - 3 < len(heads) and doubled(heads[n - 3]):
+                keys_across(*heads[n - 3])
+            if 0 <= n - 4 < len(heads) and doubled(heads[n - 4]):
+                keys_back(*heads[n - 4])

@@ -77,7 +77,7 @@ def tile_multiheadattention_pb_kernel(tc, kv_input, Wk, Wv, k_scale, cos, sin, o
         ones = keep.tile([P, P], BF16)
         nc.vector.memset(ones[:], 1.0)
         gain = keep.tile([P, 2, HALF], F32)
-        gain_swapped = keep.tile([P, 2, HALF], F32)
+        gain_signed = keep.tile([P, 2, HALF], F32)
         table_shape = [P, TILES, 2, HALF]
         same = keep.tile(table_shape, F32)
         other = keep.tile(table_shape, F32)
@@ -88,8 +88,8 @@ def tile_multiheadattention_pb_kernel(tc, kv_input, Wk, Wv, k_scale, cos, sin, o
             nc.vector.tensor_scalar_add(
                 out=gain[:].rearrange("p h c -> p (h c)"), in0=spread[:, 0:HEAD_DIM], scalar1=1.0
             )
-            nc.vector.tensor_scalar_mul(out=gain_swapped[:, 0, :], in0=gain[:, 1, :], scalar1=-1.0)
-            nc.vector.tensor_copy(out=gain_swapped[:, 1, :], in_=gain[:, 0, :])
+            nc.vector.tensor_copy(out=gain_signed[:, 0, :], in_=gain[:, 0, :])
+            nc.vector.tensor_scalar_mul(out=gain_signed[:, 1, :], in0=gain[:, 1, :], scalar1=-1.0)
             nc.vector.tensor_mul(
                 out=same[:],
                 in0=cos_bf[:].unsqueeze(2).to_broadcast(table_shape),
@@ -98,16 +98,16 @@ def tile_multiheadattention_pb_kernel(tc, kv_input, Wk, Wv, k_scale, cos, sin, o
             nc.vector.tensor_mul(
                 out=other[:],
                 in0=sin_bf[:].unsqueeze(2).to_broadcast(table_shape),
-                in1=gain_swapped[:].unsqueeze(1).to_broadcast(table_shape),
+                in1=gain_signed[:].unsqueeze(1).to_broadcast(table_shape),
             )
 
         w_codes = {}
         w_scales = {}
         w_grouped = {}
 
-        def group_weights(name, c):
-            w_grouped[name, c] = stage.tile([P, COLS * PACK], BF16, align_bytes=64, tag="w_grouped", name="w_grouped")
-            nc.vector.tensor_copy(
+        def group_weights(name, c, copy=nc.vector.tensor_copy):
+            w_grouped[name, c] = stage.tile([P, COLS * PACK], BF16, align_bytes=64, tag="w_grouped", bufs=4, name="w_grouped")
+            copy(
                 out=w_grouped[name, c][:].rearrange("p (q i t) -> p q t i", i=4, t=PACK),
                 in_=w_raw[name][:, c, :].rearrange("p (t q i) -> p q t i", t=PACK, i=4),
             )
@@ -196,10 +196,8 @@ def tile_multiheadattention_pb_kernel(tc, kv_input, Wk, Wv, k_scale, cos, sin, o
             values_finish(b, g)
 
         k_acc = {}
-        k_inv = {}
         k_straight = {}
         k_crossed = {}
-        k_sum = {}
 
         def keys_product(b, g):
             acc = project("k", b, g)
@@ -214,46 +212,41 @@ def tile_multiheadattention_pb_kernel(tc, kv_input, Wk, Wv, k_scale, cos, sin, o
             nc.scalar.activation(
                 out=inv_rms[:], in_=sum_sq[:], func=ACT.Abs_reciprocal_sqrt, bias=eps[:], scale=1.0 / HEAD_DIM
             )
-            k_inv[b, g] = inv_rms
             halves = acc[:].rearrange("p j (h c) -> p j h c", h=2)
-            straight = stage.tile(table_shape, F32)
-            nc.vector.tensor_mul(out=straight[:], in0=halves, in1=same[:])
-            crossed = stage.tile(table_shape, F32)
-            for h in range(2):
-                nc.vector.tensor_mul(out=crossed[:, :, h, :], in0=halves[:, :, 1 - h, :], in1=other[:, :, h, :])
-            k_straight[b, g] = straight
-            k_crossed[b, g] = crossed
-
-        def keys_sum(b, g):
-            roped = stage.tile([P, TILES, HEAD_DIM], F32)
-            nc.gpsimd.tensor_tensor(
-                out=roped[:].rearrange("p j d -> p (j d)"),
-                in0=k_straight[b, g][:].rearrange("p j h c -> p (j h c)"),
-                in1=k_crossed[b, g][:].rearrange("p j h c -> p (j h c)"),
-                op=mybir.AluOpType.add,
-            )
-            k_sum[b, g] = roped
+            k_straight[b, g] = stage.tile(table_shape, F32, name="k_straight")
+            k_crossed[b, g] = stage.tile(table_shape, F32, name="k_crossed")
+            for product, table in ((k_straight[b, g], same), (k_crossed[b, g], other)):
+                for j in range(TILES):
+                    nc.vector.scalar_tensor_tensor(
+                        out=product[:, j],
+                        in0=halves[:, j],
+                        scalar=inv_rms[:, j : j + 1],
+                        in1=table[:, j],
+                        op0=mybir.AluOpType.mult,
+                        op1=mybir.AluOpType.mult,
+                    )
 
         k_scaled = {}
         k_across = {}
 
-        def keys_scale(b, g, scaled):
-            for j in range(TILES):
-                nc.scalar.activation(
-                    out=scaled[:, j, :],
-                    in_=k_sum[b, g][:, j, :],
-                    func=ACT.Copy,
-                    scale=k_inv[b, g][:, j : j + 1],
+        def keys_sum(b, g, result):
+            for h in range(2):
+                half = slice(h * HALF, (h + 1) * HALF)
+                nc.gpsimd.tensor_tensor(
+                    out=result[:, :, half],
+                    in0=k_straight[b, g][:, :, h, :],
+                    in1=k_crossed[b, g][:, :, 1 - h, :],
+                    op=mybir.AluOpType.add,
                 )
 
         def keys_finish(b, g):
             k_result = results.tile([P, TILES, HEAD_DIM], F32, name="k_result_%d_%d" % (b, g))
-            keys_scale(b, g, k_result)
+            keys_sum(b, g, k_result)
             store_head(out_0, b, g, k_result[:].rearrange("p j d -> p (j d)"))
 
         def keys_scale_double(b, g):
             k_scaled[b, g] = stage.tile([P, TILES, HEAD_DIM], F32, tag="k_scaled", name="k_scaled")
-            keys_scale(b, g, k_scaled[b, g])
+            keys_sum(b, g, k_scaled[b, g])
 
         def keys_across(b, g):
             turned = psum.tile([P, TILES, P], F32, tag="bank")
@@ -261,7 +254,7 @@ def tile_multiheadattention_pb_kernel(tc, kv_input, Wk, Wv, k_scale, cos, sin, o
                 nc.tensor.transpose(turned[:, j, :], k_scaled[b, g][:, j, :], ident[:])
             k_across[b, g] = stage.tile([P, 2, TILES, COPIES, PER_COPY], F32, tag="k_across", name="k_across")
             for h in range(2):
-                nc.vector.tensor_copy(
+                nc.scalar.copy(
                     out=k_across[b, g][:, h],
                     in_=turned[:]
                     .rearrange("p j (i h) -> p h j i", h=2)[:, h]
@@ -306,21 +299,39 @@ def tile_multiheadattention_pb_kernel(tc, kv_input, Wk, Wv, k_scale, cos, sin, o
         quantise_tokens(1, 3)
         values(0, 2)
         values(0, 3)
-        quantise_weights("k")
-        for g in range(KV_HEADS):
-            values(1, g)
-        heads = [(b, g) for g in range(KV_HEADS) for b in range(BATCH)]
-        def doubled(head):
-            return head[0] == 1
-
-        for n in range(len(heads) + 4):
-            if n < len(heads):
-                keys_product(*heads[n])
-            if 1 <= n <= len(heads):
-                keys_sum(*heads[n - 1])
-            if 2 <= n < len(heads) + 2:
-                (keys_scale_double if doubled(heads[n - 2]) else keys_finish)(*heads[n - 2])
-            if 0 <= n - 3 < len(heads) and doubled(heads[n - 3]):
-                keys_across(*heads[n - 3])
-            if 0 <= n - 4 < len(heads) and doubled(heads[n - 4]):
-                keys_back(*heads[n - 4])
+        group_weights("k", 0)
+        group_weights("k", 1)
+        quantise_weights_pass("k", 0)
+        values(1, 0)
+        values(1, 1)
+        group_weights("k", 3, nc.scalar.copy)
+        group_weights("k", 2)
+        quantise_weights_pass("k", 1)
+        quantise_weights_pass("k", 3)
+        quantise_weights_pass("k", 2)
+        values(1, 2)
+        values(1, 3)
+        keys_product(0, 0)
+        keys_finish(0, 0)
+        keys_product(0, 1)
+        keys_finish(0, 1)
+        keys_product(1, 0)
+        keys_scale_double(1, 0)
+        keys_product(0, 2)
+        keys_finish(0, 2)
+        keys_product(1, 1)
+        keys_scale_double(1, 1)
+        keys_product(0, 3)
+        keys_finish(0, 3)
+        keys_across(1, 0)
+        keys_product(1, 2)
+        keys_scale_double(1, 2)
+        keys_back(1, 0)
+        keys_product(1, 3)
+        keys_scale_double(1, 3)
+        keys_across(1, 1)
+        keys_back(1, 1)
+        keys_across(1, 2)
+        keys_across(1, 3)
+        keys_back(1, 2)
+        keys_back(1, 3)

@@ -50,22 +50,33 @@ def tile_multiheadattention_pb_kernel(tc, kv_input, Wk, Wv, k_scale, cos, sin, o
         w_raw = {}
         x_raw = {}
 
-        def load_weights(name, w):
+        for name in ("v", "k"):
             w_raw[name] = keep.tile([P, PASSES, PACK * COLS], BF16, name="w_raw_" + name)
-            rows = w.rearrange("(c p t) n -> c p (t n)", p=P, t=PACK)
-            for c in range(PASSES):
-                nc.sync.dma_start(out=w_raw[name][:, c, :], in_=rows[c])
-
-        def load_batch(b):
+        for b in range(BATCH):
             x_raw[b] = keep.tile([P, TILES, FEATURES], BF16, name="x_raw_%d" % b)
-            rows = kv_input[b].rearrange("(p j) k -> p j k", j=TILES)
-            for j in range(TILES):
-                nc.sync.dma_start(out=x_raw[b][:, j, :], in_=rows[:, j, :])
 
-        load_weights("v", Wv)
-        load_batch(0)
-        load_batch(1)
-        load_weights("k", Wk)
+        def load_weights(name, w, first, last):
+            rows = w.rearrange("(c p t) n -> p c (t n)", p=P, t=PACK)
+            nc.sync.dma_start(out=w_raw[name][:, first:last, :], in_=rows[:, first:last, :])
+
+        def load_tokens(b, first, last):
+            rows = kv_input[b].rearrange("(p j) k -> p j k", j=TILES)
+            nc.sync.dma_start(out=x_raw[b][:, first:last, :], in_=rows[:, first:last, :])
+
+        load_weights("v", Wv, 0, 1)
+        load_weights("v", Wv, 1, 2)
+        load_weights("v", Wv, 2, 3)
+        load_weights("v", Wv, 3, 4)
+        load_tokens(0, 0, 1)
+        load_tokens(0, 1, 2)
+        load_tokens(0, 2, 3)
+        load_tokens(0, 3, 4)
+        load_tokens(1, 0, 1)
+        load_tokens(1, 1, 2)
+        load_tokens(1, 2, 4)
+        load_weights("k", Wk, 0, 1)
+        load_weights("k", Wk, 1, 2)
+        load_weights("k", Wk, 2, 4)
 
         ident = keep.tile([P, P], F32)
         make_identity(nc, ident[:])
@@ -227,7 +238,7 @@ def tile_multiheadattention_pb_kernel(tc, kv_input, Wk, Wv, k_scale, cos, sin, o
                     )
 
         k_scaled = {}
-        k_across = {}
+        across = {}
 
         def keys_sum(b, g, result):
             for h in range(2):
@@ -248,28 +259,51 @@ def tile_multiheadattention_pb_kernel(tc, kv_input, Wk, Wv, k_scale, cos, sin, o
             k_scaled[b, g] = stage.tile([P, TILES, HEAD_DIM], F32, tag="k_scaled", name="k_scaled")
             keys_sum(b, g, k_scaled[b, g])
 
-        def keys_across(b, g):
-            turned = psum.tile([P, TILES, P], F32, tag="bank")
-            for j in range(TILES):
-                nc.tensor.transpose(turned[:, j, :], k_scaled[b, g][:, j, :], ident[:])
-            k_across[b, g] = stage.tile([P, 2, TILES, COPIES, PER_COPY], F32, tag="k_across", name="k_across")
+        def copy_across(name, b, g, acc, copy):
+            across[name, b, g] = stage.tile([P, 2, TILES, COPIES, PER_COPY], F32, tag="across", name="across")
             for h in range(2):
-                nc.scalar.copy(
-                    out=k_across[b, g][:, h],
-                    in_=turned[:]
+                copy(
+                    out=across[name, b, g][:, h],
+                    in_=acc[:]
                     .rearrange("p j (i h) -> p h j i", h=2)[:, h]
                     .unsqueeze(2)
                     .to_broadcast([P, TILES, COPIES, PER_COPY]),
                 )
 
-        def keys_back(b, g):
-            result = results.tile([P, SLOTS, HEAD_DIM], F32, name="k_result_%d_%d" % (b, g))
-            for h, copy in enumerate((nc.scalar.copy, nc.vector.tensor_copy)):
+        def keys_across(b, g, copy=nc.scalar.copy):
+            turned = psum.tile([P, TILES, P], F32, tag="bank")
+            for j in range(TILES):
+                nc.tensor.transpose(turned[:, j, :], k_scaled[b, g][:, j, :], ident[:])
+            copy_across("k", b, g, turned, copy)
+
+        def values_across(b, g, copy=nc.scalar.copy):
+            acc = psum.tile([P, TILES, P], F32, tag="bank")
+            head_cols = slice(g * HEAD_DIM, (g + 1) * HEAD_DIM)
+            for j in range(TILES):
+                for c in range(PASSES):
+                    tokens = slice(c * P, (c + 1) * P)
+                    nc.tensor.matmul_mx(
+                        out=acc[:, j, :],
+                        lhsT=w_codes["v"][:, c, head_cols].bitcast(FP8X4),
+                        lhsT_scale=w_scales["v"][:, c, head_cols],
+                        rhs=x_codes[:, b, j, tokens].bitcast(FP8X4),
+                        rhs_scale=x_scales[:, b, j, tokens],
+                        start=(c == 0),
+                        stop=(c == PASSES - 1),
+                    )
+            copy_across("v", b, g, acc, copy)
+
+        def turn_back(name, b, g, copies=(nc.scalar.copy, nc.vector.tensor_copy)):
+            result = results.tile([P, SLOTS, HEAD_DIM], F32, name="%s_result_%d_%d" % (name, b, g))
+            for h, copy in enumerate(copies):
                 back = psum.tile([P, TILES, HEAD_DIM], F32, tag="bank")
                 for j in range(TILES):
-                    nc.tensor.transpose(back[:, j, :], k_across[b, g][:, h, j].rearrange("p r i -> p (r i)"), ident[:])
+                    nc.tensor.transpose(
+                        back[:, j, :], across[name, b, g][:, h, j].rearrange("p r i -> p (r i)"), ident[:]
+                    )
                 copy(out=result[:, h * TILES : (h + 1) * TILES, :], in_=back[:])
-            served = out_0[b, g * REPEAT : (g + 1) * REPEAT].rearrange("(q r) t d -> q (r t d)", r=COPIES)
+            out = out_1 if name == "v" else out_0
+            served = out[b, g * REPEAT : (g + 1) * REPEAT].rearrange("(q r) t d -> q (r t d)", r=COPIES)
             run = SLOTS * HEAD_DIM
             nc.sync.dma_start(
                 out=served.rearrange("q (p e) -> p q e", e=run),
@@ -282,36 +316,37 @@ def tile_multiheadattention_pb_kernel(tc, kv_input, Wk, Wv, k_scale, cos, sin, o
             group_tokens(0, j)
             quantise_tokens(0, j)
         flip_tokens(1, 0)
-        flip_tokens(1, 1)
         group_tokens(1, 0)
+        quantise_tokens(1, 0)
+        build_tables()
         values_product(0, 0)
         values_finish(0, 0)
+        flip_tokens(1, 1)
         group_tokens(1, 1)
-        quantise_tokens(1, 0)
+        group_weights("k", 0)
         quantise_tokens(1, 1)
         values(0, 1)
-        build_tables()
         flip_tokens(1, 2)
         group_tokens(1, 2)
         flip_tokens(1, 3)
         group_tokens(1, 3)
+        group_weights("k", 1)
         quantise_tokens(1, 2)
+        quantise_weights_pass("k", 0)
         quantise_tokens(1, 3)
         values(0, 2)
         values(0, 3)
-        group_weights("k", 0)
-        group_weights("k", 1)
-        quantise_weights_pass("k", 0)
-        values(1, 0)
-        values(1, 1)
         group_weights("k", 3, nc.scalar.copy)
         group_weights("k", 2)
         quantise_weights_pass("k", 1)
-        quantise_weights_pass("k", 3)
         quantise_weights_pass("k", 2)
+        quantise_weights_pass("k", 3)
+        values(1, 0)
+        values(1, 1)
         values(1, 2)
-        values(1, 3)
+        values_across(1, 3)
         keys_product(0, 0)
+        turn_back("v", 1, 3)
         keys_finish(0, 0)
         keys_product(0, 1)
         keys_finish(0, 1)
@@ -322,16 +357,18 @@ def tile_multiheadattention_pb_kernel(tc, kv_input, Wk, Wv, k_scale, cos, sin, o
         keys_product(1, 1)
         keys_scale_double(1, 1)
         keys_product(0, 3)
-        keys_finish(0, 3)
+        keys_scale_double(0, 3)
         keys_across(1, 0)
         keys_product(1, 2)
         keys_scale_double(1, 2)
-        keys_back(1, 0)
+        turn_back("k", 1, 0)
         keys_product(1, 3)
         keys_scale_double(1, 3)
         keys_across(1, 1)
-        keys_back(1, 1)
+        keys_across(0, 3)
+        turn_back("k", 1, 1)
         keys_across(1, 2)
+        turn_back("k", 0, 3)
         keys_across(1, 3)
-        keys_back(1, 2)
-        keys_back(1, 3)
+        turn_back("k", 1, 2)
+        turn_back("k", 1, 3)

@@ -65,8 +65,7 @@ def tile_multiheadattention_pb_kernel(tc, kv_input, Wk, Wv, k_scale, cos, sin, o
 
         load_weights("v", Wv, 0, 1)
         load_weights("v", Wv, 1, 2)
-        load_weights("v", Wv, 2, 3)
-        load_weights("v", Wv, 3, 4)
+        load_weights("v", Wv, 2, 4)
         load_tokens(0, 0, 1)
         load_tokens(0, 1, 2)
         load_tokens(0, 2, 3)
@@ -90,8 +89,7 @@ def tile_multiheadattention_pb_kernel(tc, kv_input, Wk, Wv, k_scale, cos, sin, o
         gain = keep.tile([P, 2, HALF], F32)
         gain_signed = keep.tile([P, 2, HALF], F32)
         table_shape = [P, TILES, 2, HALF]
-        same = keep.tile(table_shape, F32)
-        other = keep.tile(table_shape, F32)
+        rope = keep.tile([P, TILES, 2, HEAD_DIM], F32)
 
         def build_tables():
             spread = psum.tile([P, COLS], F32, tag="bank")
@@ -101,16 +99,12 @@ def tile_multiheadattention_pb_kernel(tc, kv_input, Wk, Wv, k_scale, cos, sin, o
             )
             nc.vector.tensor_copy(out=gain_signed[:, 0, :], in_=gain[:, 0, :])
             nc.vector.tensor_scalar_mul(out=gain_signed[:, 1, :], in0=gain[:, 1, :], scalar1=-1.0)
-            nc.vector.tensor_mul(
-                out=same[:],
-                in0=cos_bf[:].unsqueeze(2).to_broadcast(table_shape),
-                in1=gain[:].unsqueeze(1).to_broadcast(table_shape),
-            )
-            nc.vector.tensor_mul(
-                out=other[:],
-                in0=sin_bf[:].unsqueeze(2).to_broadcast(table_shape),
-                in1=gain_signed[:].unsqueeze(1).to_broadcast(table_shape),
-            )
+            for kind, (angles, factors) in enumerate(((cos_bf, gain), (sin_bf, gain_signed))):
+                nc.vector.tensor_mul(
+                    out=rope[:, :, kind, :].rearrange("p j (h c) -> p j h c", h=2),
+                    in0=angles[:].unsqueeze(2).to_broadcast(table_shape),
+                    in1=factors[:].unsqueeze(1).to_broadcast(table_shape),
+                )
 
         w_codes = {}
         w_scales = {}
@@ -207,8 +201,7 @@ def tile_multiheadattention_pb_kernel(tc, kv_input, Wk, Wv, k_scale, cos, sin, o
             values_finish(b, g)
 
         k_acc = {}
-        k_straight = {}
-        k_crossed = {}
+        k_products = {}
 
         def keys_product(b, g):
             acc = project("k", b, g)
@@ -223,30 +216,27 @@ def tile_multiheadattention_pb_kernel(tc, kv_input, Wk, Wv, k_scale, cos, sin, o
             nc.scalar.activation(
                 out=inv_rms[:], in_=sum_sq[:], func=ACT.Abs_reciprocal_sqrt, bias=eps[:], scale=1.0 / HEAD_DIM
             )
-            halves = acc[:].rearrange("p j (h c) -> p j h c", h=2)
-            k_straight[b, g] = stage.tile(table_shape, F32, name="k_straight")
-            k_crossed[b, g] = stage.tile(table_shape, F32, name="k_crossed")
-            for product, table in ((k_straight[b, g], same), (k_crossed[b, g], other)):
-                for j in range(TILES):
-                    nc.vector.scalar_tensor_tensor(
-                        out=product[:, j],
-                        in0=halves[:, j],
-                        scalar=inv_rms[:, j : j + 1],
-                        in1=table[:, j],
-                        op0=mybir.AluOpType.mult,
-                        op1=mybir.AluOpType.mult,
-                    )
+            k_products[b, g] = stage.tile([P, TILES, 2, HEAD_DIM], F32, name="k_products")
+            for j in range(TILES):
+                nc.vector.scalar_tensor_tensor(
+                    out=k_products[b, g][:, j],
+                    in0=acc[:, j, :].unsqueeze(1).to_broadcast([P, 2, HEAD_DIM]),
+                    scalar=inv_rms[:, j : j + 1],
+                    in1=rope[:, j],
+                    op0=mybir.AluOpType.mult,
+                    op1=mybir.AluOpType.mult,
+                )
 
         k_scaled = {}
         across = {}
 
         def keys_sum(b, g, result):
-            for h in range(2):
-                half = slice(h * HALF, (h + 1) * HALF)
+            low, high = slice(0, HALF), slice(HALF, HEAD_DIM)
+            for half, other_half in ((low, high), (high, low)):
                 nc.gpsimd.tensor_tensor(
                     out=result[:, :, half],
-                    in0=k_straight[b, g][:, :, h, :],
-                    in1=k_crossed[b, g][:, :, 1 - h, :],
+                    in0=k_products[b, g][:, :, 0, half],
+                    in1=k_products[b, g][:, :, 1, other_half],
                     op=mybir.AluOpType.add,
                 )
 
@@ -261,14 +251,13 @@ def tile_multiheadattention_pb_kernel(tc, kv_input, Wk, Wv, k_scale, cos, sin, o
 
         def copy_across(name, b, g, acc, copy):
             across[name, b, g] = stage.tile([P, 2, TILES, COPIES, PER_COPY], F32, tag="across", name="across")
-            for h in range(2):
-                copy(
-                    out=across[name, b, g][:, h],
-                    in_=acc[:]
-                    .rearrange("p j (i h) -> p h j i", h=2)[:, h]
-                    .unsqueeze(2)
-                    .to_broadcast([P, TILES, COPIES, PER_COPY]),
-                )
+            copy(
+                out=across[name, b, g][:],
+                in_=acc[:]
+                .rearrange("p j (i h) -> p h j i", h=2)
+                .unsqueeze(3)
+                .to_broadcast([P, 2, TILES, COPIES, PER_COPY]),
+            )
 
         def keys_across(b, g, copy=nc.scalar.copy):
             turned = psum.tile([P, TILES, P], F32, tag="bank")
@@ -346,29 +335,31 @@ def tile_multiheadattention_pb_kernel(tc, kv_input, Wk, Wv, k_scale, cos, sin, o
         values(1, 2)
         values_across(1, 3)
         keys_product(0, 0)
-        turn_back("v", 1, 3)
         keys_finish(0, 0)
         keys_product(0, 1)
-        keys_finish(0, 1)
+        turn_back("v", 1, 3)
+        keys_scale_double(0, 1)
+        keys_product(0, 2)
+        keys_scale_double(0, 2)
+        keys_product(0, 3)
+        keys_finish(0, 3)
         keys_product(1, 0)
         keys_scale_double(1, 0)
-        keys_product(0, 2)
-        keys_finish(0, 2)
+        keys_across(0, 1)
         keys_product(1, 1)
         keys_scale_double(1, 1)
-        keys_product(0, 3)
-        keys_scale_double(0, 3)
-        keys_across(1, 0)
+        keys_across(0, 2)
+        turn_back("k", 0, 1)
         keys_product(1, 2)
         keys_scale_double(1, 2)
-        turn_back("k", 1, 0)
+        turn_back("k", 0, 2)
         keys_product(1, 3)
         keys_scale_double(1, 3)
+        keys_across(1, 0)
         keys_across(1, 1)
-        keys_across(0, 3)
-        turn_back("k", 1, 1)
+        turn_back("k", 1, 0)
         keys_across(1, 2)
-        turn_back("k", 0, 3)
+        turn_back("k", 1, 1)
         keys_across(1, 3)
         turn_back("k", 1, 2)
         turn_back("k", 1, 3)

@@ -249,23 +249,21 @@ def tile_multiheadattention_pb_kernel(tc, kv_input, Wk, Wv, k_scale, cos, sin, o
             k_scaled[b, g] = stage.tile([P, TILES, HEAD_DIM], F32, tag="k_scaled", name="k_scaled")
             keys_sum(b, g, k_scaled[b, g])
 
-        def copy_across(name, b, g, acc, copy):
-            across[name, b, g] = stage.tile([P, 2, TILES, COPIES, PER_COPY], F32, tag="across", name="across")
+        def copy_across(name, b, g, acc, copy, copies):
+            shape = [P, copies, TILES, copies, P // copies]
+            across[name, b, g] = stage.tile(shape, F32, tag="across_%d" % copies, bufs=6 // copies, name="across")
             copy(
                 out=across[name, b, g][:],
-                in_=acc[:]
-                .rearrange("p j (i h) -> p h j i", h=2)
-                .unsqueeze(3)
-                .to_broadcast([P, 2, TILES, COPIES, PER_COPY]),
+                in_=acc[:].rearrange("p j (i h) -> p h j i", h=copies).unsqueeze(3).to_broadcast(shape),
             )
 
-        def keys_across(b, g, copy=nc.scalar.copy):
+        def keys_across(b, g, copy=nc.scalar.copy, copies=2):
             turned = psum.tile([P, TILES, P], F32, tag="bank")
             for j in range(TILES):
                 nc.tensor.transpose(turned[:, j, :], k_scaled[b, g][:, j, :], ident[:])
-            copy_across("k", b, g, turned, copy)
+            copy_across("k", b, g, turned, copy, copies)
 
-        def values_across(b, g, copy=nc.scalar.copy):
+        def values_across(b, g, copy=nc.scalar.copy, copies=2):
             acc = psum.tile([P, TILES, P], F32, tag="bank")
             head_cols = slice(g * HEAD_DIM, (g + 1) * HEAD_DIM)
             for j in range(TILES):
@@ -280,23 +278,24 @@ def tile_multiheadattention_pb_kernel(tc, kv_input, Wk, Wv, k_scale, cos, sin, o
                         start=(c == 0),
                         stop=(c == PASSES - 1),
                     )
-            copy_across("v", b, g, acc, copy)
+            copy_across("v", b, g, acc, copy, copies)
 
-        def turn_back(name, b, g, copies=(nc.scalar.copy, nc.vector.tensor_copy)):
-            result = results.tile([P, SLOTS, HEAD_DIM], F32, name="%s_result_%d_%d" % (name, b, g))
-            for h, copy in enumerate(copies):
+        def turn_back(name, b, g, engines=(nc.scalar.copy, nc.vector.tensor_copy)):
+            copies = across[name, b, g].shape[1]
+            result = results.tile([P, copies * TILES, HEAD_DIM], F32, name="%s_result_%d_%d" % (name, b, g))
+            for h in range(copies):
                 back = psum.tile([P, TILES, HEAD_DIM], F32, tag="bank")
                 for j in range(TILES):
                     nc.tensor.transpose(
                         back[:, j, :], across[name, b, g][:, h, j].rearrange("p r i -> p (r i)"), ident[:]
                     )
-                copy(out=result[:, h * TILES : (h + 1) * TILES, :], in_=back[:])
+                engines[h % 2](out=result[:, h * TILES : (h + 1) * TILES, :], in_=back[:])
             out = out_1 if name == "v" else out_0
-            served = out[b, g * REPEAT : (g + 1) * REPEAT].rearrange("(q r) t d -> q (r t d)", r=COPIES)
-            run = SLOTS * HEAD_DIM
+            served = out[b, g * REPEAT : (g + 1) * REPEAT].rearrange("(q r) t d -> q (r t d)", r=copies)
+            run = copies * TILES * HEAD_DIM
             nc.sync.dma_start(
                 out=served.rearrange("q (p e) -> p q e", e=run),
-                in_=result[:].rearrange("p j d -> p (j d)").unsqueeze(1).to_broadcast([P, REPEAT // COPIES, run]),
+                in_=result[:].rearrange("p j d -> p (j d)").unsqueeze(1).to_broadcast([P, REPEAT // copies, run]),
             )
 
         quantise_weights("v")
@@ -333,7 +332,7 @@ def tile_multiheadattention_pb_kernel(tc, kv_input, Wk, Wv, k_scale, cos, sin, o
         values(1, 0)
         values(1, 1)
         values(1, 2)
-        values_across(1, 3)
+        values_across(1, 3, nc.vector.tensor_copy)
         keys_product(0, 0)
         keys_finish(0, 0)
         keys_product(0, 1)
@@ -360,6 +359,6 @@ def tile_multiheadattention_pb_kernel(tc, kv_input, Wk, Wv, k_scale, cos, sin, o
         turn_back("k", 1, 0)
         keys_across(1, 2)
         turn_back("k", 1, 1)
-        keys_across(1, 3)
+        keys_across(1, 3, copies=4)
         turn_back("k", 1, 2)
         turn_back("k", 1, 3)

from contextlib import ExitStack

import concourse.mybir as mybir
from concourse.masks import make_identity

F32 = mybir.dt.float32
BF16 = mybir.dt.bfloat16
U32 = mybir.dt.uint32
U8 = mybir.dt.uint8
FP8X4 = mybir.dt.float8_e4m3fn_x4
ACT = mybir.ActivationFunctionType

BATCH, TOKENS, FEATURES = 2, 512, 2048
KV_HEADS, HEAD_DIM, REPEAT = 4, 128, 4
HALF = HEAD_DIM // 2
EPS = 1e-6

P = 128
PACK = 4
K_PASS = P * PACK
PASSES = FEATURES // K_PASS
TILES = TOKENS // P
COPIES = 2
PER_COPY = P // COPIES
SLOTS = TOKENS // PER_COPY
COLS = KV_HEADS * HEAD_DIM
PAIRS = PACK // 2

FLOPS = 2 * BATCH * TOKENS * FEATURES * 2 * COLS


def tile_multiheadattention_pb_kernel(tc, kv_input, Wk, Wv, k_scale, cos, sin, out_0, out_1):
    nc = tc.nc
    with ExitStack() as ctx:
        keep = ctx.enter_context(tc.tile_pool(name="keep", bufs=1))
        stage = ctx.enter_context(tc.tile_pool(name="stage", bufs=3))
        small = ctx.enter_context(tc.tile_pool(name="small", bufs=4))
        results = ctx.enter_context(tc.tile_pool(name="results", bufs=1))
        psum = ctx.enter_context(tc.psum_pool(name="psum", bufs=8))
        ctx.enter_context(tc.manual_schedule())

        cos_bf = keep.tile([P, TILES, HALF], BF16)
        sin_bf = keep.tile([P, TILES, HALF], BF16)
        nc.scalar.dma_start(out=cos_bf[:], in_=cos.rearrange("(p j) c -> p j c", j=TILES))
        nc.scalar.dma_start(out=sin_bf[:], in_=sin.rearrange("(p j) c -> p j c", j=TILES))
        scale_rows = keep.tile([P, HEAD_DIM], BF16)
        nc.vector.memset(scale_rows[:], 0.0)
        nc.scalar.dma_start(out=scale_rows[0:1, :], in_=k_scale.rearrange("(o d) -> o d", o=1))

        w_raw = {}
        x_raw = {}

        for name in ("v", "k"):
            w_raw[name] = keep.tile([P, PASSES, PACK * COLS], BF16, name="w_raw_" + name)
        for b in range(BATCH):
            x_raw[b] = keep.tile([P, TILES, FEATURES], BF16, name="x_raw_%d" % b)

        def load_weights(name, w, first, last):
            rows = w.rearrange("(c p t) n -> p c (t n)", p=P, t=PACK)
            nc.sync.dma_start(out=w_raw[name][:, first:last, :], in_=rows[:, first:last, :])

        def load_tokens(b, first, last):
            rows = kv_input[b].rearrange("(p j) k -> p j k", j=TILES)
            nc.sync.dma_start(out=x_raw[b][:, first:last, :], in_=rows[:, first:last, :])

        load_weights("v", Wv, 0, 1)
        load_weights("v", Wv, 1, 2)
        load_weights("v", Wv, 2, 4)
        load_tokens(0, 0, 1)
        load_tokens(0, 1, 2)
        load_tokens(0, 2, 3)
        load_tokens(0, 3, 4)
        load_tokens(1, 0, 1)
        load_tokens(1, 1, 2)
        load_tokens(1, 2, 4)
        load_weights("k", Wk, 0, 1)
        load_weights("k", Wk, 1, 2)
        load_weights("k", Wk, 2, 4)

        ident = keep.tile([P, P], F32)
        make_identity(nc, ident[:])
        eps = keep.tile([P, 1], F32)
        nc.vector.memset(eps[:], EPS)
        warm = keep.tile([P, 1], F32)
        nc.scalar.activation(out=warm[:], in_=eps[:], func=ACT.Abs_reciprocal_sqrt)

        ones = keep.tile([P, P], BF16)
        nc.vector.memset(ones[:], 1.0)
        gain = keep.tile([P, 2, HALF], F32)
        gain_signed = keep.tile([P, 2, HALF], F32)
        table_shape = [P, TILES, 2, HALF]
        rope = keep.tile([P, TILES, 2, HEAD_DIM], F32)

        def build_tables():
            spread = psum.tile([P, COLS], F32, tag="bank")
            nc.tensor.matmul(out=spread[:, 0:HEAD_DIM], lhsT=ones[:], rhs=scale_rows[:], start=True, stop=True)
            nc.vector.tensor_scalar_add(
                out=gain[:].rearrange("p h c -> p (h c)"), in0=spread[:, 0:HEAD_DIM], scalar1=1.0
            )
            nc.vector.tensor_copy(out=gain_signed[:, 0, :], in_=gain[:, 0, :])
            nc.vector.tensor_scalar_mul(out=gain_signed[:, 1, :], in0=gain[:, 1, :], scalar1=-1.0)
            for kind, (angles, factors) in enumerate(((cos_bf, gain), (sin_bf, gain_signed))):
                nc.vector.tensor_mul(
                    out=rope[:, :, kind, :].rearrange("p j (h c) -> p j h c", h=2),
                    in0=angles[:].unsqueeze(2).to_broadcast(table_shape),
                    in1=factors[:].unsqueeze(1).to_broadcast(table_shape),
                )

        w_codes = {}
        w_scales = {}
        w_grouped = {}

        def group_weights(name, c, copy=nc.vector.tensor_copy):
            w_grouped[name, c] = stage.tile([P, COLS * PACK], BF16, align_bytes=64, tag="w_grouped", bufs=4, name="w_grouped")
            copy(
                out=w_grouped[name, c][:].rearrange("p (q i t) -> p q t i", i=4, t=PACK),
                in_=w_raw[name][:, c, :].rearrange("p (t q i) -> p q t i", t=PACK, i=4),
            )

        def quantise_weights_pass(name, c):
            nc.vector.quantize_mx(
                out=w_codes[name][:, c, :].bitcast(FP8X4),
                scales=w_scales[name][:, c, :],
                in_=w_grouped[name, c][:],
            )

        for name in ("v", "k"):
            w_codes[name] = keep.tile([P, PASSES, COLS], U32, name="w_codes_" + name, align_bytes=64)
            w_scales[name] = keep.tile([P, PASSES, COLS], U8, name="w_scales_" + name, align_bytes=64)

        def quantise_weights(name):
            group_weights(name, 0)
            for c in range(PASSES):
                if c + 1 < PASSES:
                    group_weights(name, c + 1)
                quantise_weights_pass(name, c)

        x_codes = keep.tile([P, BATCH, TILES, PASSES * P], U32, align_bytes=64)
        x_scales = keep.tile([P, BATCH, TILES, PASSES * P], U8, align_bytes=64)

        passes_per_bank = COLS // (PAIRS * P)
        x_flipped = {}
        x_grouped = {}

        def flip_tokens(b, j):
            words = x_raw[b][:, j, :].bitcast(F32).rearrange("p (c i u) -> p c u i", c=PASSES, u=PAIRS)
            for c0 in range(0, PASSES, passes_per_bank):
                flipped = psum.tile([P, passes_per_bank, PAIRS, P], F32, tag="bank")
                x_flipped[b, j, c0] = flipped
                for cc in range(passes_per_bank):
                    for u in range(PAIRS):
                        nc.tensor.transpose(flipped[:, cc, u, :], words[:, c0 + cc, u, :], ident[:])

        def group_tokens(b, j):
            x_grouped[b, j] = stage.tile([P, PASSES * P * PACK], BF16, align_bytes=64, tag="x_grouped", name="x_grouped")
            grouped_words = x_grouped[b, j][:].bitcast(F32).rearrange("p (c m u) -> p c m u", c=PASSES, u=PAIRS)
            for c0 in range(0, PASSES, passes_per_bank):
                nc.scalar.copy(
                    out=grouped_words[:, c0 : c0 + passes_per_bank, :, :],
                    in_=x_flipped[b, j, c0][:].rearrange("p c u m -> p c m u"),
                )

        def quantise_tokens(b, j):
            nc.vector.quantize_mx(
                out=x_codes[:, b, j, :].bitcast(FP8X4), scales=x_scales[:, b, j, :], in_=x_grouped[b, j][:]
            )

        def project(name, b, g):
            acc = psum.tile([P, TILES, HEAD_DIM], F32, tag="bank")
            head_cols = slice(g * HEAD_DIM, (g + 1) * HEAD_DIM)
            for j in range(TILES):
                for c in range(PASSES):
                    tokens = slice(c * P, (c + 1) * P)
                    nc.tensor.matmul_mx(
                        out=acc[:, j, :],
                        lhsT=x_codes[:, b, j, tokens].bitcast(FP8X4),
                        lhsT_scale=x_scales[:, b, j, tokens],
                        rhs=w_codes[name][:, c, head_cols].bitcast(FP8X4),
                        rhs_scale=w_scales[name][:, c, head_cols],
                        start=(c == 0),
                        stop=(c == PASSES - 1),
                    )
            return acc

        def store_head(out, b, g, result):
            served = out[b, g * REPEAT : (g + 1) * REPEAT].rearrange("r (p j) d -> p r (j d)", j=TILES)
            nc.sync.dma_start(out=served, in_=result.unsqueeze(1).to_broadcast([P, REPEAT, TILES * HEAD_DIM]))

        v_acc = {}

        def values_product(b, g):
            v_acc[b, g] = project("v", b, g)

        def values_finish(b, g):
            v_result = results.tile([P, TILES * HEAD_DIM], F32, name="v_result_%d_%d" % (b, g))
            nc.scalar.copy(out=v_result[:], in_=v_acc[b, g][:].rearrange("p j d -> p (j d)"))
            store_head(out_1, b, g, v_result[:])

        def values(b, g):
            values_product(b, g)
            values_finish(b, g)

        k_acc = {}
        k_products = {}

        def keys_product(b, g):
            acc = project("k", b, g)
            k_acc[b, g] = acc
            sum_sq = small.tile([P, TILES], F32)
            for j in range(TILES):
                squares = stage.tile([P, HEAD_DIM], F32)
                nc.scalar.activation(
                    out=squares[:], in_=acc[:, j, :], func=ACT.Square, accum_out=sum_sq[:, j : j + 1]
                )
            inv_rms = small.tile([P, TILES], F32)
            nc.scalar.activation(
                out=inv_rms[:], in_=sum_sq[:], func=ACT.Abs_reciprocal_sqrt, bias=eps[:], scale=1.0 / HEAD_DIM
            )
            k_products[b, g] = stage.tile([P, TILES, 2, HEAD_DIM], F32, name="k_products")
            for j in range(TILES):
                nc.vector.scalar_tensor_tensor(
                    out=k_products[b, g][:, j],
                    in0=acc[:, j, :].unsqueeze(1).to_broadcast([P, 2, HEAD_DIM]),
                    scalar=inv_rms[:, j : j + 1],
                    in1=rope[:, j],
                    op0=mybir.AluOpType.mult,
                    op1=mybir.AluOpType.mult,
                )

        k_scaled = {}
        across = {}

        def keys_sum(b, g, result):
            low, high = slice(0, HALF), slice(HALF, HEAD_DIM)
            for half, other_half in ((low, high), (high, low)):
                nc.gpsimd.tensor_tensor(
                    out=result[:, :, half],
                    in0=k_products[b, g][:, :, 0, half],
                    in1=k_products[b, g][:, :, 1, other_half],
                    op=mybir.AluOpType.add,
                )

        def keys_finish(b, g):
            k_result = results.tile([P, TILES, HEAD_DIM], F32, name="k_result_%d_%d" % (b, g))
            keys_sum(b, g, k_result)
            store_head(out_0, b, g, k_result[:].rearrange("p j d -> p (j d)"))

        def keys_scale_double(b, g):
            k_scaled[b, g] = stage.tile([P, TILES, HEAD_DIM], F32, tag="k_scaled", name="k_scaled")
            keys_sum(b, g, k_scaled[b, g])

        def copy_across(name, b, g, acc, copy, copies):
            shape = [P, copies, TILES, copies, P // copies]
            across[name, b, g] = stage.tile(shape, F32, tag="across_%d" % copies, bufs=6 // copies, name="across")
            copy(
                out=across[name, b, g][:],
                in_=acc[:].rearrange("p j (i h) -> p h j i", h=copies).unsqueeze(3).to_broadcast(shape),
            )

        def keys_across(b, g, copy=nc.scalar.copy, copies=2):
            turned = psum.tile([P, TILES, P], F32, tag="bank")
            for j in range(TILES):
                nc.tensor.transpose(turned[:, j, :], k_scaled[b, g][:, j, :], ident[:])
            copy_across("k", b, g, turned, copy, copies)

        def values_across(b, g, copy=nc.scalar.copy, copies=2):
            acc = psum.tile([P, TILES, P], F32, tag="bank")
            head_cols = slice(g * HEAD_DIM, (g + 1) * HEAD_DIM)
            for j in range(TILES):
                for c in range(PASSES):
                    tokens = slice(c * P, (c + 1) * P)
                    nc.tensor.matmul_mx(
                        out=acc[:, j, :],
                        lhsT=w_codes["v"][:, c, head_cols].bitcast(FP8X4),
                        lhsT_scale=w_scales["v"][:, c, head_cols],
                        rhs=x_codes[:, b, j, tokens].bitcast(FP8X4),
                        rhs_scale=x_scales[:, b, j, tokens],
                        start=(c == 0),
                        stop=(c == PASSES - 1),
                    )
            copy_across("v", b, g, acc, copy, copies)

        def turn_back(name, b, g, engines=(nc.scalar.copy, nc.vector.tensor_copy)):
            copies = across[name, b, g].shape[1]
            result = results.tile([P, copies * TILES, HEAD_DIM], F32, name="%s_result_%d_%d" % (name, b, g))
            for h in range(copies):
                back = psum.tile([P, TILES, HEAD_DIM], F32, tag="bank")
                for j in range(TILES):
                    nc.tensor.transpose(
                        back[:, j, :], across[name, b, g][:, h, j].rearrange("p r i -> p (r i)"), ident[:]
                    )
                engines[h % 2](out=result[:, h * TILES : (h + 1) * TILES, :], in_=back[:])
            out = out_1 if name == "v" else out_0
            served = out[b, g * REPEAT : (g + 1) * REPEAT].rearrange("(q r) t d -> q (r t d)", r=copies)
            run = copies * TILES * HEAD_DIM
            nc.sync.dma_start(
                out=served.rearrange("q (p e) -> p q e", e=run),
                in_=result[:].rearrange("p j d -> p (j d)").unsqueeze(1).to_broadcast([P, REPEAT // copies, run]),
            )

        quantise_weights("v")
        for j in range(TILES):
            flip_tokens(0, j)
            group_tokens(0, j)
            quantise_tokens(0, j)
        flip_tokens(1, 0)
        group_tokens(1, 0)
        quantise_tokens(1, 0)
        build_tables()
        values_product(0, 0)
        values_finish(0, 0)
        flip_tokens(1, 1)
        group_tokens(1, 1)
        group_weights("k", 0)
        quantise_tokens(1, 1)
        values(0, 1)
        flip_tokens(1, 2)
        group_tokens(1, 2)
        flip_tokens(1, 3)
        group_tokens(1, 3)
        group_weights("k", 1)
        quantise_tokens(1, 2)
        quantise_weights_pass("k", 0)
        quantise_tokens(1, 3)
        values(0, 2)
        values(0, 3)
        group_weights("k", 3, nc.scalar.copy)
        group_weights("k", 2)
        quantise_weights_pass("k", 1)
        quantise_weights_pass("k", 2)
        quantise_weights_pass("k", 3)
        values(1, 0)
        values(1, 1)
        values(1, 2)
        values_across(1, 3, nc.vector.tensor_copy)
        keys_product(0, 0)
        keys_finish(0, 0)
        keys_product(0, 1)
        turn_back("v", 1, 3)
        keys_scale_double(0, 1)
        keys_product(0, 2)
        keys_scale_double(0, 2)
        keys_product(0, 3)
        keys_finish(0, 3)
        keys_product(1, 0)
        keys_scale_double(1, 0)
        keys_across(0, 1)
        keys_product(1, 1)
        keys_scale_double(1, 1)
        keys_across(0, 2)
        turn_back("k", 0, 1)
        keys_product(1, 2)
        keys_scale_double(1, 2)
        turn_back("k", 0, 2)
        keys_product(1, 3)
        keys_scale_double(1, 3)
        keys_across(1, 0)
        keys_across(1, 1)
        turn_back("k", 1, 0)
        keys_across(1, 2)
        turn_back("k", 1, 1)
        keys_across(1, 3, copies=4)
        turn_back("k", 1, 2)
        turn_back("k", 1, 3)
